import numpy as np
import ml_dtypes

BF16 = ml_dtypes.bfloat16


def bf(x):
    return np.asarray(x, np.float32).astype(BF16)


def f32(x):
    return np.asarray(x, np.float32)


def f64(x):
    return np.asarray(x).astype(np.float64)


def striped(idx):
    return np.tile(idx.reshape(-1, 16).T, (8, 1))


D, S, M, N = 128, 1024, 512, 512


def sigmoid(v):
    return 1.0 / (1.0 + np.exp(-v))


def setup_inputs():
    return {"table": bf(np.random.standard_normal((D, S))), "w": bf(np.random.standard_normal((D, M)) / np.sqrt(2.0 * D)), "b": f32(0.2 * np.random.standard_normal((M, 1))), "dur": f32(np.random.uniform(size=(1, N))), "offs": striped(np.random.permutation(np.tile(np.arange(S), 2))[:N])}


def reference(table, w, b, dur, offs):
    idx = offs[:16].T.reshape(-1)
    p = f64(w).T @ f64(table)[:, idx] + f64(b)
    p_in, p_z, p_inbar, p_decay = p.reshape(-1, D, p.shape[1])
    z = np.tanh(p_z)
    c = sigmoid(p_in) * z
    cbar = sigmoid(p_inbar) * z
    delta = np.log(1.0 + np.exp(p_decay))
    return cbar + (c - cbar) * np.exp(-delta * f64(dur))

@@ -1,0 +1,80 @@
+import concourse.mybir as mybir
+
+D, S, N = 128, 1024, 512
+GATE_IN, GATE_Z, GATE_INBAR, GATE_DECAY = 0, 1, 2, 3
+GATES = 4
+FLOPS = 2 * D * GATES * D * N
+
+BF16, F32, U16 = mybir.dt.bfloat16, mybir.dt.float32, mybir.dt.uint16
+ACT = mybir.ActivationFunctionType
+ALU = mybir.AluOpType
+
+LN_FLOOR = 1e-19
+
+
+def tile_ctlstm_kernel(tc, table, w, b, dur, offs, out):
+    nc = tc.nc
+    with (
+        tc.tile_pool(name="held", bufs=1) as held,
+        tc.psum_pool(name="psum", bufs=1) as psum,
+    ):
+        offsets = held.tile([D, N // 16], U16, name="offsets")
+        nc.sync.dma_start(offsets[:], offs)
+        table_sb = held.tile([D, S], BF16, name="table_sb")
+        nc.sync.dma_start(table_sb[:], table)
+        w_sb = held.tile([D, GATES * D], BF16, name="w_sb")
+        nc.scalar.dma_start(w_sb[:], w)
+        bias = held.tile([D, GATES], F32, name="bias")
+        with nc.allow_non_contiguous_dma(reason="512 floats, one to a partition and gate"):
+            nc.gpsimd.dma_start(bias[:], b.rearrange("(g h) o -> h (g o)", g=GATES))
+        dur_sb = held.tile([D, N], F32, name="dur_sb")
+        nc.gpsimd.dma_start(dur_sb[:], dur.broadcast_to([D, N]))
+
+        picked = table_sb[:].indirect(offsets[:])
+        p = {}
+        for g in (GATE_Z, GATE_IN, GATE_INBAR, GATE_DECAY):
+            p[g] = psum.tile([D, N], F32, name=f"p{g}")
+            nc.tensor.matmul(p[g][:], w_sb[:, g * D : (g + 1) * D], picked)
+
+        z = held.tile([D, N], F32, name="z")
+        nc.scalar.activation(z[:], p[GATE_Z][:], ACT.Tanh, bias=bias[:, GATE_Z : GATE_Z + 1])
+        s_in = held.tile([D, N], F32, name="s_in")
+        nc.scalar.activation(s_in[:], p[GATE_IN][:], ACT.Sigmoid, bias=bias[:, GATE_IN : GATE_IN + 1])
+        s_inbar = held.tile([D, N], F32, name="s_inbar")
+        nc.scalar.activation(
+            s_inbar[:], p[GATE_INBAR][:], ACT.Sigmoid, bias=bias[:, GATE_INBAR : GATE_INBAR + 1]
+        )
+        s_decay = held.tile([D, N], F32, name="s_decay")
+        nc.scalar.activation(
+            s_decay[:], p[GATE_DECAY][:], ACT.Sigmoid, bias=bias[:, GATE_DECAY : GATE_DECAY + 1]
+        )
+
+        log_s = held.tile([D, N], F32, name="log_s")
+        nc.scalar.activation(log_s[:], s_decay[:], ACT.Ln, bias=LN_FLOOR)
+
+        c = held.tile([D, N], F32, name="c")
+        nc.vector.tensor_mul(c[:], s_in[:], z[:])
+        cbar = held.tile([D, N], F32, name="cbar")
+        nc.vector.tensor_mul(cbar[:], s_inbar[:], z[:])
+        gap = held.tile([D, N], F32, name="gap")
+        nc.vector.tensor_sub(gap[:], c[:], cbar[:])
+
+        delta = held.tile([D, N], F32, name="delta")
+        nc.vector.scalar_tensor_tensor(
+            delta[:],
+            p[GATE_DECAY][:],
+            bias[:, GATE_DECAY : GATE_DECAY + 1],
+            log_s[:],
+            op0=ALU.add,
+            op1=ALU.subtract,
+        )
+        decay = held.tile([D, N], F32, name="decay")
+        nc.vector.scalar_tensor_tensor(decay[:], delta[:], 0.0, dur_sb[:], op0=ALU.max, op1=ALU.mult)
+        fade = held.tile([D, N], F32, name="fade")
+        nc.scalar.activation(fade[:], decay[:], ACT.Exp, scale=-1.0)
+
+        faded = held.tile([D, N], F32, name="faded")
+        nc.vector.tensor_mul(faded[:], gap[:], fade[:])
+        result = held.tile([D, N], F32, name="result")
+        nc.vector.tensor_add(result[:], faded[:], cbar[:])
+        nc.sync.dma_start(out, result[:])

@@ -30,20 +30,24 @@ def tile_ctlstm_kernel(tc, table, w, b, dur, offs, out):
         dur_sb = held.tile([D, N], F32, name="dur_sb")
         nc.gpsimd.dma_start(dur_sb[:], dur.broadcast_to([D, N]))
 
+        warm = held.tile([D, 1], F32, name="warm")
+        nc.vector.memset(warm[:], 0.0)
+        nc.scalar.activation(warm[:], warm[:], ACT.Sigmoid)
+
         picked = table_sb[:].indirect(offsets[:])
         p = {}
-        for g in (GATE_Z, GATE_IN, GATE_INBAR, GATE_DECAY):
+        for g in (GATE_IN, GATE_INBAR, GATE_Z, GATE_DECAY):
             p[g] = psum.tile([D, N], F32, name=f"p{g}")
             nc.tensor.matmul(p[g][:], w_sb[:, g * D : (g + 1) * D], picked)
 
-        z = held.tile([D, N], F32, name="z")
-        nc.scalar.activation(z[:], p[GATE_Z][:], ACT.Tanh, bias=bias[:, GATE_Z : GATE_Z + 1])
         s_in = held.tile([D, N], F32, name="s_in")
         nc.scalar.activation(s_in[:], p[GATE_IN][:], ACT.Sigmoid, bias=bias[:, GATE_IN : GATE_IN + 1])
         s_inbar = held.tile([D, N], F32, name="s_inbar")
         nc.scalar.activation(
             s_inbar[:], p[GATE_INBAR][:], ACT.Sigmoid, bias=bias[:, GATE_INBAR : GATE_INBAR + 1]
         )
+        z = held.tile([D, N], F32, name="z")
+        nc.scalar.activation(z[:], p[GATE_Z][:], ACT.Tanh, bias=bias[:, GATE_Z : GATE_Z + 1])
         s_decay = held.tile([D, N], F32, name="s_decay")
         nc.scalar.activation(
             s_decay[:], p[GATE_DECAY][:], ACT.Sigmoid, bias=bias[:, GATE_DECAY : GATE_DECAY + 1]

@@ -1,4 +1,5 @@
 import concourse.mybir as mybir
+from concourse.masks import make_identity
 
 D, S, N = 128, 1024, 512
 GATE_IN, GATE_Z, GATE_INBAR, GATE_DECAY = 0, 1, 2, 3
@@ -20,15 +21,21 @@ def tile_ctlstm_kernel(tc, table, w, b, dur, offs, out):
     ):
         offsets = held.tile([D, N // 16], U16, name="offsets")
         nc.sync.dma_start(offsets[:], offs)
+        b_rows = held.tile([GATES, D], F32, name="b_rows")
+        nc.sync.dma_start(b_rows[:], b.rearrange("(g h) o -> g (h o)", g=GATES))
         table_sb = held.tile([D, S], BF16, name="table_sb")
         nc.sync.dma_start(table_sb[:], table)
         w_sb = held.tile([D, GATES * D], BF16, name="w_sb")
         nc.scalar.dma_start(w_sb[:], w)
-        bias = held.tile([D, GATES], F32, name="bias")
-        with nc.allow_non_contiguous_dma(reason="512 floats, one to a partition and gate"):
-            nc.gpsimd.dma_start(bias[:], b.rearrange("(g h) o -> h (g o)", g=GATES))
         dur_sb = held.tile([D, N], F32, name="dur_sb")
-        nc.gpsimd.dma_start(dur_sb[:], dur.broadcast_to([D, N]))
+        nc.sync.dma_start(dur_sb[:], dur.broadcast_to([D, N]))
+
+        ident = held.tile([GATES, GATES], F32, name="ident")
+        make_identity(nc, ident[:])
+        bias_ps = psum.tile([D, GATES], F32, name="bias_ps")
+        nc.tensor.matmul(bias_ps[:], b_rows[:], ident[:])
+        bias = held.tile([D, GATES], F32, name="bias")
+        nc.vector.tensor_copy(bias[:], bias_ps[:])
 
         warm = held.tile([D, 1], F32, name="warm")
         nc.vector.memset(warm[:], 0.0)

@@ -1,5 +1,4 @@
 import concourse.mybir as mybir
-from concourse.masks import make_identity
 
 D, S, N = 128, 1024, 512
 GATE_IN, GATE_Z, GATE_INBAR, GATE_DECAY = 0, 1, 2, 3
@@ -9,6 +8,8 @@ FLOPS = 2 * D * GATES * D * N
 BF16, F32, U16 = mybir.dt.bfloat16, mybir.dt.float32, mybir.dt.uint16
 ACT = mybir.ActivationFunctionType
 ALU = mybir.AluOpType
+
+WARM_MATMULS = 6
 
 LN_FLOOR = 1e-19
 
@@ -21,25 +22,25 @@ def tile_ctlstm_kernel(tc, table, w, b, dur, offs, out):
     ):
         offsets = held.tile([D, N // 16], U16, name="offsets")
         nc.sync.dma_start(offsets[:], offs)
-        b_rows = held.tile([GATES, D], F32, name="b_rows")
-        nc.sync.dma_start(b_rows[:], b.rearrange("(g h) o -> g (h o)", g=GATES))
         table_sb = held.tile([D, S], BF16, name="table_sb")
         nc.sync.dma_start(table_sb[:], table)
         w_sb = held.tile([D, GATES * D], BF16, name="w_sb")
         nc.scalar.dma_start(w_sb[:], w)
-        dur_sb = held.tile([D, N], F32, name="dur_sb")
-        nc.sync.dma_start(dur_sb[:], dur.broadcast_to([D, N]))
-
-        ident = held.tile([GATES, GATES], F32, name="ident")
-        make_identity(nc, ident[:])
-        bias_ps = psum.tile([D, GATES], F32, name="bias_ps")
-        nc.tensor.matmul(bias_ps[:], b_rows[:], ident[:])
         bias = held.tile([D, GATES], F32, name="bias")
-        nc.vector.tensor_copy(bias[:], bias_ps[:])
+        with nc.allow_non_contiguous_dma(reason="512 floats, one to a partition and gate"):
+            nc.gpsimd.dma_start(bias[:], b.rearrange("(g h) o -> h (g o)", g=GATES))
+        dur_sb = held.tile([D, N], F32, name="dur_sb")
+        nc.gpsimd.dma_start(dur_sb[:], dur.broadcast_to([D, N]))
 
         warm = held.tile([D, 1], F32, name="warm")
         nc.vector.memset(warm[:], 0.0)
         nc.scalar.activation(warm[:], warm[:], ACT.Sigmoid)
+
+        zeros = held.tile([D, N], BF16, name="zeros")
+        nc.vector.memset(zeros[:], 0.0)
+        idle = psum.tile([D, N], F32, name="idle")
+        for k in range(WARM_MATMULS):
+            nc.tensor.matmul(idle[:], zeros[:, :D], zeros[:])
 
         picked = table_sb[:].indirect(offsets[:])
         p = {}

@@ -3,15 +3,17 @@ import concourse.mybir as mybir
 D, S, N = 128, 1024, 512
 GATE_IN, GATE_Z, GATE_INBAR, GATE_DECAY = 0, 1, 2, 3
 GATES = 4
+PIECES = 2
+W = N // PIECES
 FLOPS = 2 * D * GATES * D * N
 
 BF16, F32, U16 = mybir.dt.bfloat16, mybir.dt.float32, mybir.dt.uint16
 ACT = mybir.ActivationFunctionType
 ALU = mybir.AluOpType
 
-WARM_MATMULS = 6
-
-LN_FLOOR = 1e-19
+Q_LEAD = 0.04134767
+Q_SHIFT_1, Q_REST_1 = -2.22530212, 1.66203741
+Q_SHIFT_2, Q_REST_2 = 0.32158366, 3.55303458
 
 
 def tile_ctlstm_kernel(tc, table, w, b, dur, offs, out):
@@ -22,71 +24,85 @@ def tile_ctlstm_kernel(tc, table, w, b, dur, offs, out):
     ):
         offsets = held.tile([D, N // 16], U16, name="offsets")
         nc.sync.dma_start(offsets[:], offs)
+        w_sb = held.tile([D, GATES * D], BF16, name="w_sb")
+        nc.sync.dma_start(w_sb[:], w)
         table_sb = held.tile([D, S], BF16, name="table_sb")
         nc.sync.dma_start(table_sb[:], table)
-        w_sb = held.tile([D, GATES * D], BF16, name="w_sb")
-        nc.scalar.dma_start(w_sb[:], w)
+        dur_sb = held.tile([D, N], F32, name="dur_sb")
+        nc.sync.dma_start(dur_sb[:], dur.broadcast_to([D, N]))
         bias = held.tile([D, GATES], F32, name="bias")
         with nc.allow_non_contiguous_dma(reason="512 floats, one to a partition and gate"):
-            nc.gpsimd.dma_start(bias[:], b.rearrange("(g h) o -> h (g o)", g=GATES))
-        dur_sb = held.tile([D, N], F32, name="dur_sb")
-        nc.gpsimd.dma_start(dur_sb[:], dur.broadcast_to([D, N]))
+            nc.scalar.dma_start(bias[:], b.rearrange("(g h) o -> h (g o)", g=GATES))
 
         warm = held.tile([D, 1], F32, name="warm")
         nc.vector.memset(warm[:], 0.0)
-        nc.scalar.activation(warm[:], warm[:], ACT.Sigmoid)
+        nc.scalar.activation(warm[:], warm[:], ACT.Exp)
 
-        zeros = held.tile([D, N], BF16, name="zeros")
-        nc.vector.memset(zeros[:], 0.0)
-        idle = psum.tile([D, N], F32, name="idle")
-        for k in range(WARM_MATMULS):
-            nc.tensor.matmul(idle[:], zeros[:, :D], zeros[:])
+        half_bias = held.tile([D, GATES], F32, name="half_bias")
+        nc.vector.tensor_scalar_mul(half_bias[:], bias[:], 0.5)
 
-        picked = table_sb[:].indirect(offsets[:])
+        def column(tile, g):
+            return tile[:, g : g + 1]
+
+        def pieces_of(tile):
+            return [tile[:, k * W : (k + 1) * W] for k in range(PIECES)]
+
+        def fresh(name):
+            return pieces_of(held.tile([D, N], F32, name=name))
+
+        def on_scalar(name, in_, func, bias=0.0, scale=1.0):
+            res = fresh(name)
+            for k in range(PIECES):
+                nc.scalar.activation(res[k], in_[k], func, bias=bias, scale=scale)
+            return res
+
+        def on_vector(name, in0, scalar, in1, op0, op1):
+            res = fresh(name)
+            for k in range(PIECES):
+                nc.vector.scalar_tensor_tensor(res[k], in0[k], scalar, in1[k], op0=op0, op1=op1)
+            return res
+
+        def on_vector_plain(name, in0, in1, op):
+            res = fresh(name)
+            for k in range(PIECES):
+                nc.vector.tensor_tensor(res[k], in0[k], in1[k], op)
+            return res
+
         p = {}
-        for g in (GATE_IN, GATE_INBAR, GATE_Z, GATE_DECAY):
-            p[g] = psum.tile([D, N], F32, name=f"p{g}")
-            nc.tensor.matmul(p[g][:], w_sb[:, g * D : (g + 1) * D], picked)
+        for g in (GATE_DECAY, GATE_IN, GATE_INBAR, GATE_Z):
+            p[g] = []
+            for k in range(PIECES):
+                bank = psum.tile([D, W], F32, name=f"p{g}_{k}")
+                picked = table_sb[:].indirect(offsets[:, k * W // 16 : (k + 1) * W // 16])
+                nc.tensor.matmul(bank[:], w_sb[:, g * D : (g + 1) * D], picked)
+                p[g].append(bank[:])
 
-        s_in = held.tile([D, N], F32, name="s_in")
-        nc.scalar.activation(s_in[:], p[GATE_IN][:], ACT.Sigmoid, bias=bias[:, GATE_IN : GATE_IN + 1])
-        s_inbar = held.tile([D, N], F32, name="s_inbar")
-        nc.scalar.activation(
-            s_inbar[:], p[GATE_INBAR][:], ACT.Sigmoid, bias=bias[:, GATE_INBAR : GATE_INBAR + 1]
+        dur_pieces = pieces_of(dur_sb)
+        y_abs = on_scalar("y_abs", p[GATE_DECAY], ACT.Abs, bias=column(bias, GATE_DECAY))
+        y_pos = fresh("y_pos")
+        for k in range(PIECES):
+            nc.vector.tensor_scalar(
+                y_pos[k], p[GATE_DECAY][k], column(bias, GATE_DECAY), 0.0, op0=ALU.add, op1=ALU.max
+            )
+        t = on_scalar("t", y_abs, ACT.Exp, scale=-1.0)
+        y_pos_dur = on_vector_plain("y_pos_dur", y_pos, dur_pieces, ALU.mult)
+        square_1 = on_scalar("square_1", t, ACT.Square, bias=Q_SHIFT_1)
+        square_2 = on_scalar("square_2", t, ACT.Square, bias=Q_SHIFT_2)
+        t_dur = on_vector_plain("t_dur", t, dur_pieces, ALU.mult)
+        one_factor = on_vector("one_factor", square_1, Q_REST_1, t_dur, ALU.add, ALU.mult)
+        both_factors = on_vector("both_factors", square_2, Q_REST_2, one_factor, ALU.add, ALU.mult)
+        x = on_vector("x", both_factors, Q_LEAD, y_pos_dur, ALU.mult, ALU.add)
+
+        tanh_in = on_scalar("tanh_in", p[GATE_IN], ACT.Tanh, bias=column(half_bias, GATE_IN), scale=0.5)
+        tanh_inbar = on_scalar(
+            "tanh_inbar", p[GATE_INBAR], ACT.Tanh, bias=column(half_bias, GATE_INBAR), scale=0.5
         )
-        z = held.tile([D, N], F32, name="z")
-        nc.scalar.activation(z[:], p[GATE_Z][:], ACT.Tanh, bias=bias[:, GATE_Z : GATE_Z + 1])
-        s_decay = held.tile([D, N], F32, name="s_decay")
-        nc.scalar.activation(
-            s_decay[:], p[GATE_DECAY][:], ACT.Sigmoid, bias=bias[:, GATE_DECAY : GATE_DECAY + 1]
-        )
+        gap = on_vector_plain("gap", tanh_in, tanh_inbar, ALU.subtract)
+        fade = on_scalar("fade", x, ACT.Exp, scale=-1.0)
+        z = on_scalar("z", p[GATE_Z], ACT.Tanh, bias=column(bias, GATE_Z))
 
-        log_s = held.tile([D, N], F32, name="log_s")
-        nc.scalar.activation(log_s[:], s_decay[:], ACT.Ln, bias=LN_FLOOR)
-
-        c = held.tile([D, N], F32, name="c")
-        nc.vector.tensor_mul(c[:], s_in[:], z[:])
-        cbar = held.tile([D, N], F32, name="cbar")
-        nc.vector.tensor_mul(cbar[:], s_inbar[:], z[:])
-        gap = held.tile([D, N], F32, name="gap")
-        nc.vector.tensor_sub(gap[:], c[:], cbar[:])
-
-        delta = held.tile([D, N], F32, name="delta")
-        nc.vector.scalar_tensor_tensor(
-            delta[:],
-            p[GATE_DECAY][:],
-            bias[:, GATE_DECAY : GATE_DECAY + 1],
-            log_s[:],
-            op0=ALU.add,
-            op1=ALU.subtract,
-        )
-        decay = held.tile([D, N], F32, name="decay")
-        nc.vector.scalar_tensor_tensor(decay[:], delta[:], 0.0, dur_sb[:], op0=ALU.max, op1=ALU.mult)
-        fade = held.tile([D, N], F32, name="fade")
-        nc.scalar.activation(fade[:], decay[:], ACT.Exp, scale=-1.0)
-
-        faded = held.tile([D, N], F32, name="faded")
-        nc.vector.tensor_mul(faded[:], gap[:], fade[:])
-        result = held.tile([D, N], F32, name="result")
-        nc.vector.tensor_add(result[:], faded[:], cbar[:])
-        nc.sync.dma_start(out, result[:])
+        faded = on_vector_plain("faded", gap, fade, ALU.mult)
+        gate = on_vector("gate", tanh_inbar, 1.0, faded, ALU.add, ALU.add)
+        result = on_vector("result", gate, 0.5, z, ALU.mult, ALU.mult)
+        for k in range(PIECES):
+            nc.sync.dma_start(out[:, k * W : (k + 1) * W], result[k])

@@ -3,7 +3,7 @@ import concourse.mybir as mybir
 D, S, N = 128, 1024, 512
 GATE_IN, GATE_Z, GATE_INBAR, GATE_DECAY = 0, 1, 2, 3
 GATES = 4
-PIECES = 2
+PIECES = 4
 W = N // PIECES
 FLOPS = 2 * D * GATES * D * N
 
@@ -24,12 +24,12 @@ def tile_ctlstm_kernel(tc, table, w, b, dur, offs, out):
     ):
         offsets = held.tile([D, N // 16], U16, name="offsets")
         nc.sync.dma_start(offsets[:], offs)
-        w_sb = held.tile([D, GATES * D], BF16, name="w_sb")
-        nc.sync.dma_start(w_sb[:], w)
         table_sb = held.tile([D, S], BF16, name="table_sb")
         nc.sync.dma_start(table_sb[:], table)
         dur_sb = held.tile([D, N], F32, name="dur_sb")
         nc.sync.dma_start(dur_sb[:], dur.broadcast_to([D, N]))
+        w_sb = held.tile([D, GATES * D], BF16, name="w_sb")
+        nc.scalar.dma_start(w_sb[:], w)
         bias = held.tile([D, GATES], F32, name="bias")
         with nc.allow_non_contiguous_dma(reason="512 floats, one to a partition and gate"):
             nc.scalar.dma_start(bias[:], b.rearrange("(g h) o -> h (g o)", g=GATES))
@@ -68,14 +68,19 @@ def tile_ctlstm_kernel(tc, table, w, b, dur, offs, out):
                 nc.vector.tensor_tensor(res[k], in0[k], in1[k], op)
             return res
 
-        p = {}
-        for g in (GATE_DECAY, GATE_IN, GATE_INBAR, GATE_Z):
-            p[g] = []
-            for k in range(PIECES):
-                bank = psum.tile([D, W], F32, name=f"p{g}_{k}")
-                picked = table_sb[:].indirect(offsets[:, k * W // 16 : (k + 1) * W // 16])
-                nc.tensor.matmul(bank[:], w_sb[:, g * D : (g + 1) * D], picked)
-                p[g].append(bank[:])
+        def w_block(g):
+            return w_sb[:, g * D : (g + 1) * D]
+
+        p = {GATE_DECAY: []}
+        for k in range(PIECES):
+            bank = psum.tile([D, W], F32, name=f"p_decay_{k}")
+            picked = table_sb[:].indirect(offsets[:, k * W // 16 : (k + 1) * W // 16])
+            nc.tensor.matmul(bank[:], w_block(GATE_DECAY), picked)
+            p[GATE_DECAY].append(bank[:])
+        for g in (GATE_IN, GATE_INBAR, GATE_Z):
+            bank = psum.tile([D, N], F32, name=f"p{g}")
+            nc.tensor.matmul(bank[:], w_block(g), table_sb[:].indirect(offsets[:]))
+            p[g] = pieces_of(bank)
 
         dur_pieces = pieces_of(dur_sb)
         y_abs = on_scalar("y_abs", p[GATE_DECAY], ACT.Abs, bias=column(bias, GATE_DECAY))

@@ -3,7 +3,8 @@ import concourse.mybir as mybir
 D, S, N = 128, 1024, 512
 GATE_IN, GATE_Z, GATE_INBAR, GATE_DECAY = 0, 1, 2, 3
 GATES = 4
-PIECES = 4
+BLOCK = 32
+PIECES = 2
 W = N // PIECES
 FLOPS = 2 * D * GATES * D * N
 
@@ -26,20 +27,24 @@ def tile_ctlstm_kernel(tc, table, w, b, dur, offs, out):
         nc.sync.dma_start(offsets[:], offs)
         table_sb = held.tile([D, S], BF16, name="table_sb")
         nc.sync.dma_start(table_sb[:], table)
-        dur_sb = held.tile([D, N], F32, name="dur_sb")
-        nc.sync.dma_start(dur_sb[:], dur.broadcast_to([D, N]))
         w_sb = held.tile([D, GATES * D], BF16, name="w_sb")
         nc.scalar.dma_start(w_sb[:], w)
-        bias = held.tile([D, GATES], F32, name="bias")
-        with nc.allow_non_contiguous_dma(reason="512 floats, one to a partition and gate"):
-            nc.scalar.dma_start(bias[:], b.rearrange("(g h) o -> h (g o)", g=GATES))
+        b_runs = held.tile([D, BLOCK], F32, name="b_runs", align_bytes=64)
+        nc.gpsimd.memset(b_runs[:], 0.0)
+        b_view = b.rearrange("(g q i) o -> q g (i o)", g=GATES, i=BLOCK)
+        for q in range(D // BLOCK):
+            nc.sync.dma_start(b_runs[q * BLOCK : q * BLOCK + GATES, :], b_view[q])
+        dur_sb = held.tile([D, N], F32, name="dur_sb")
+        nc.sync.dma_start(dur_sb[:], dur.broadcast_to([D, N]))
 
         warm = held.tile([D, 1], F32, name="warm")
         nc.vector.memset(warm[:], 0.0)
         nc.scalar.activation(warm[:], warm[:], ACT.Exp)
 
+        bias = held.tile([D, BLOCK], F32, name="bias", align_bytes=64)
+        nc.vector.transpose(bias[:], b_runs[:])
         half_bias = held.tile([D, GATES], F32, name="half_bias")
-        nc.vector.tensor_scalar_mul(half_bias[:], bias[:], 0.5)
+        nc.vector.tensor_scalar_mul(half_bias[:], bias[:, :GATES], 0.5)
 
         def column(tile, g):
             return tile[:, g : g + 1]
@@ -68,19 +73,14 @@ def tile_ctlstm_kernel(tc, table, w, b, dur, offs, out):
                 nc.vector.tensor_tensor(res[k], in0[k], in1[k], op)
             return res
 
-        def w_block(g):
-            return w_sb[:, g * D : (g + 1) * D]
-
-        p = {GATE_DECAY: []}
-        for k in range(PIECES):
-            bank = psum.tile([D, W], F32, name=f"p_decay_{k}")
-            picked = table_sb[:].indirect(offsets[:, k * W // 16 : (k + 1) * W // 16])
-            nc.tensor.matmul(bank[:], w_block(GATE_DECAY), picked)
-            p[GATE_DECAY].append(bank[:])
-        for g in (GATE_IN, GATE_INBAR, GATE_Z):
-            bank = psum.tile([D, N], F32, name=f"p{g}")
-            nc.tensor.matmul(bank[:], w_block(g), table_sb[:].indirect(offsets[:]))
-            p[g] = pieces_of(bank)
+        p = {}
+        for g in (GATE_DECAY, GATE_IN, GATE_INBAR, GATE_Z):
+            p[g] = []
+            for k in range(PIECES):
+                bank = psum.tile([D, W], F32, name=f"p{g}_{k}")
+                picked = table_sb[:].indirect(offsets[:, k * W // 16 : (k + 1) * W // 16])
+                nc.tensor.matmul(bank[:], w_sb[:, g * D : (g + 1) * D], picked)
+                p[g].append(bank[:])
 
         dur_pieces = pieces_of(dur_sb)
         y_abs = on_scalar("y_abs", p[GATE_DECAY], ACT.Abs, bias=column(bias, GATE_DECAY))

@@ -1,20 +1,24 @@
 import concourse.mybir as mybir
 
-D, S, N = 128, 1024, 512
-GATE_IN, GATE_Z, GATE_INBAR, GATE_DECAY = 0, 1, 2, 3
+D = 128
+TYPES = 1024
+N = 512
+PER_COLUMN = 16
 GATES = 4
-BLOCK = 32
-PIECES = 2
-W = N // PIECES
+GATE_IN, GATE_Z, GATE_INBAR, GATE_DECAY = 0, 1, 2, 3
 FLOPS = 2 * D * GATES * D * N
 
-BF16, F32, U16 = mybir.dt.bfloat16, mybir.dt.float32, mybir.dt.uint16
-ACT = mybir.ActivationFunctionType
-ALU = mybir.AluOpType
+PSUM_BANKS = 8
+PIECES = PSUM_BANKS // GATES
+PIECE = N // PIECES
 
 Q_LEAD = 0.04134767
 Q_SHIFT_1, Q_REST_1 = -2.22530212, 1.66203741
 Q_SHIFT_2, Q_REST_2 = 0.32158366, 3.55303458
+
+BF16, F32, U16 = mybir.dt.bfloat16, mybir.dt.float32, mybir.dt.uint16
+ACT = mybir.ActivationFunctionType
+ALU = mybir.AluOpType
 
 
 def tile_ctlstm_kernel(tc, table, w, b, dur, offs, out):
@@ -23,91 +27,88 @@ def tile_ctlstm_kernel(tc, table, w, b, dur, offs, out):
         tc.tile_pool(name="held", bufs=1) as held,
         tc.psum_pool(name="psum", bufs=1) as psum,
     ):
-        offsets = held.tile([D, N // 16], U16, name="offsets")
+        offsets = held.tile([D, N // PER_COLUMN], U16, name="offsets")
         nc.sync.dma_start(offsets[:], offs)
-        table_sb = held.tile([D, S], BF16, name="table_sb")
-        nc.sync.dma_start(table_sb[:], table)
         w_sb = held.tile([D, GATES * D], BF16, name="w_sb")
-        nc.scalar.dma_start(w_sb[:], w)
-        b_runs = held.tile([D, BLOCK], F32, name="b_runs", align_bytes=64)
-        nc.gpsimd.memset(b_runs[:], 0.0)
-        b_view = b.rearrange("(g q i) o -> q g (i o)", g=GATES, i=BLOCK)
-        for q in range(D // BLOCK):
-            nc.sync.dma_start(b_runs[q * BLOCK : q * BLOCK + GATES, :], b_view[q])
+        nc.sync.dma_start(w_sb[:], w)
+        table_sb = held.tile([D, TYPES], BF16, name="table_sb")
+        nc.sync.dma_start(table_sb[:], table)
         dur_sb = held.tile([D, N], F32, name="dur_sb")
         nc.sync.dma_start(dur_sb[:], dur.broadcast_to([D, N]))
+        b_sb = held.tile([D, GATES], F32, name="b_sb")
+        with nc.allow_non_contiguous_dma(reason="512 floats, one to a partition and gate"):
+            nc.scalar.dma_start(b_sb[:], b.rearrange("(g h) o -> h (g o)", g=GATES))
 
-        warm = held.tile([D, 1], F32, name="warm")
-        nc.vector.memset(warm[:], 0.0)
-        nc.scalar.activation(warm[:], warm[:], ACT.Exp)
+        scratch = held.tile([D, 1], F32, name="scratch")
+        nc.vector.memset(scratch[:], 0.0)
+        nc.scalar.activation(scratch[:], scratch[:], ACT.Exp)
 
-        bias = held.tile([D, BLOCK], F32, name="bias", align_bytes=64)
-        nc.vector.transpose(bias[:], b_runs[:])
-        half_bias = held.tile([D, GATES], F32, name="half_bias")
-        nc.vector.tensor_scalar_mul(half_bias[:], bias[:, :GATES], 0.5)
+        half_b_sb = held.tile([D, GATES], F32, name="half_b_sb")
+        nc.vector.tensor_scalar_mul(half_b_sb[:], b_sb[:], 0.5)
 
         def column(tile, g):
             return tile[:, g : g + 1]
 
         def pieces_of(tile):
-            return [tile[:, k * W : (k + 1) * W] for k in range(PIECES)]
+            return [tile[:, k * PIECE : (k + 1) * PIECE] for k in range(PIECES)]
 
         def fresh(name):
             return pieces_of(held.tile([D, N], F32, name=name))
 
         def on_scalar(name, in_, func, bias=0.0, scale=1.0):
-            res = fresh(name)
+            made = fresh(name)
             for k in range(PIECES):
-                nc.scalar.activation(res[k], in_[k], func, bias=bias, scale=scale)
-            return res
+                nc.scalar.activation(made[k], in_[k], func, bias=bias, scale=scale)
+            return made
 
-        def on_vector(name, in0, scalar, in1, op0, op1):
-            res = fresh(name)
+        def on_vector(name, in0, op, in1):
+            made = fresh(name)
             for k in range(PIECES):
-                nc.vector.scalar_tensor_tensor(res[k], in0[k], scalar, in1[k], op0=op0, op1=op1)
-            return res
+                nc.vector.tensor_tensor(made[k], in0[k], in1[k], op)
+            return made
 
-        def on_vector_plain(name, in0, in1, op):
-            res = fresh(name)
+        def on_vector_fused(name, in0, op0, scalar, op1, in1):
+            made = fresh(name)
             for k in range(PIECES):
-                nc.vector.tensor_tensor(res[k], in0[k], in1[k], op)
-            return res
+                nc.vector.scalar_tensor_tensor(made[k], in0[k], scalar, in1[k], op0=op0, op1=op1)
+            return made
 
         p = {}
         for g in (GATE_DECAY, GATE_IN, GATE_INBAR, GATE_Z):
             p[g] = []
             for k in range(PIECES):
-                bank = psum.tile([D, W], F32, name=f"p{g}_{k}")
-                picked = table_sb[:].indirect(offsets[:, k * W // 16 : (k + 1) * W // 16])
+                bank = psum.tile([D, PIECE], F32, name=f"p{g}_{k}")
+                columns = slice(k * PIECE // PER_COLUMN, (k + 1) * PIECE // PER_COLUMN)
+                picked = table_sb[:].indirect(offsets[:, columns])
                 nc.tensor.matmul(bank[:], w_sb[:, g * D : (g + 1) * D], picked)
                 p[g].append(bank[:])
 
         dur_pieces = pieces_of(dur_sb)
-        y_abs = on_scalar("y_abs", p[GATE_DECAY], ACT.Abs, bias=column(bias, GATE_DECAY))
+        y_abs = on_scalar("y_abs", p[GATE_DECAY], ACT.Abs, bias=column(b_sb, GATE_DECAY))
         y_pos = fresh("y_pos")
         for k in range(PIECES):
             nc.vector.tensor_scalar(
-                y_pos[k], p[GATE_DECAY][k], column(bias, GATE_DECAY), 0.0, op0=ALU.add, op1=ALU.max
+                y_pos[k], p[GATE_DECAY][k], column(b_sb, GATE_DECAY), 0.0, op0=ALU.add, op1=ALU.max
             )
         t = on_scalar("t", y_abs, ACT.Exp, scale=-1.0)
-        y_pos_dur = on_vector_plain("y_pos_dur", y_pos, dur_pieces, ALU.mult)
+        y_pos_dur = on_vector("y_pos_dur", y_pos, ALU.mult, dur_pieces)
         square_1 = on_scalar("square_1", t, ACT.Square, bias=Q_SHIFT_1)
         square_2 = on_scalar("square_2", t, ACT.Square, bias=Q_SHIFT_2)
-        t_dur = on_vector_plain("t_dur", t, dur_pieces, ALU.mult)
-        one_factor = on_vector("one_factor", square_1, Q_REST_1, t_dur, ALU.add, ALU.mult)
-        both_factors = on_vector("both_factors", square_2, Q_REST_2, one_factor, ALU.add, ALU.mult)
-        x = on_vector("x", both_factors, Q_LEAD, y_pos_dur, ALU.mult, ALU.add)
+        t_dur = on_vector("t_dur", t, ALU.mult, dur_pieces)
+        one_factor = on_vector_fused("one_factor", square_1, ALU.add, Q_REST_1, ALU.mult, t_dur)
+        both_factors = on_vector_fused("both_factors", square_2, ALU.add, Q_REST_2, ALU.mult, one_factor)
+        x = on_vector_fused("x", both_factors, ALU.mult, Q_LEAD, ALU.add, y_pos_dur)
 
-        tanh_in = on_scalar("tanh_in", p[GATE_IN], ACT.Tanh, bias=column(half_bias, GATE_IN), scale=0.5)
+        tanh_in = on_scalar("tanh_in", p[GATE_IN], ACT.Tanh, bias=column(half_b_sb, GATE_IN), scale=0.5)
         tanh_inbar = on_scalar(
-            "tanh_inbar", p[GATE_INBAR], ACT.Tanh, bias=column(half_bias, GATE_INBAR), scale=0.5
+            "tanh_inbar", p[GATE_INBAR], ACT.Tanh, bias=column(half_b_sb, GATE_INBAR), scale=0.5
         )
-        gap = on_vector_plain("gap", tanh_in, tanh_inbar, ALU.subtract)
+        gap = on_vector("gap", tanh_in, ALU.subtract, tanh_inbar)
         fade = on_scalar("fade", x, ACT.Exp, scale=-1.0)
-        z = on_scalar("z", p[GATE_Z], ACT.Tanh, bias=column(bias, GATE_Z))
+        z = on_scalar("z", p[GATE_Z], ACT.Tanh, bias=column(b_sb, GATE_Z))
 
-        faded = on_vector_plain("faded", gap, fade, ALU.mult)
-        gate = on_vector("gate", tanh_inbar, 1.0, faded, ALU.add, ALU.add)
-        result = on_vector("result", gate, 0.5, z, ALU.mult, ALU.mult)
+        faded = on_vector("faded", gap, ALU.mult, fade)
+        mix = on_vector_fused("mix", tanh_inbar, ALU.add, 1.0, ALU.add, faded)
+        result = on_vector_fused("result", mix, ALU.mult, 0.5, ALU.mult, z)
         for k in range(PIECES):
-            nc.sync.dma_start(out[:, k * W : (k + 1) * W], result[k])
+            nc.sync.dma_start(out[:, k * PIECE : (k + 1) * PIECE], result[k])

@@ -12,9 +12,8 @@ PSUM_BANKS = 8
 PIECES = PSUM_BANKS // GATES
 PIECE = N // PIECES
 
-Q_LEAD = 0.04134767
-Q_SHIFT_1, Q_REST_1 = -2.22530212, 1.66203741
-Q_SHIFT_2, Q_REST_2 = 0.32158366, 3.55303458
+SHIFT = 0.44068679
+Q_SCALE, Q_SHIFT, Q_REST = 0.37062380, -0.20779434, 1.18033029
 
 BF16, F32, U16 = mybir.dt.bfloat16, mybir.dt.float32, mybir.dt.uint16
 ACT = mybir.ActivationFunctionType
@@ -85,19 +84,12 @@ def tile_ctlstm_kernel(tc, table, w, b, dur, offs, out):
 
         dur_pieces = pieces_of(dur_sb)
         y_abs = on_scalar("y_abs", p[GATE_DECAY], ACT.Abs, bias=column(b_sb, GATE_DECAY))
-        y_pos = fresh("y_pos")
-        for k in range(PIECES):
-            nc.vector.tensor_scalar(
-                y_pos[k], p[GATE_DECAY][k], column(b_sb, GATE_DECAY), 0.0, op0=ALU.add, op1=ALU.max
-            )
-        t = on_scalar("t", y_abs, ACT.Exp, scale=-1.0)
-        y_pos_dur = on_vector("y_pos_dur", y_pos, ALU.mult, dur_pieces)
-        square_1 = on_scalar("square_1", t, ACT.Square, bias=Q_SHIFT_1)
-        square_2 = on_scalar("square_2", t, ACT.Square, bias=Q_SHIFT_2)
-        t_dur = on_vector("t_dur", t, ALU.mult, dur_pieces)
-        one_factor = on_vector_fused("one_factor", square_1, ALU.add, Q_REST_1, ALU.mult, t_dur)
-        both_factors = on_vector_fused("both_factors", square_2, ALU.add, Q_REST_2, ALU.mult, one_factor)
-        x = on_vector_fused("x", both_factors, ALU.mult, Q_LEAD, ALU.add, y_pos_dur)
+        y_dur = on_vector_fused("y_dur", p[GATE_DECAY], ALU.add, column(b_sb, GATE_DECAY), ALU.mult, dur_pieces)
+        tau = on_scalar("tau", y_abs, ACT.Tanh, bias=SHIFT, scale=0.5)
+        square = on_scalar("square", tau, ACT.Square, bias=Q_SHIFT, scale=Q_SCALE)
+        minus_line_dur = on_vector_fused("minus_line_dur", tau, ALU.add, -1.0, ALU.mult, dur_pieces)
+        minus_log_dur = on_vector_fused("minus_log_dur", square, ALU.add, Q_REST, ALU.mult, minus_line_dur)
+        x = on_vector_fused("x", y_dur, ALU.max, 0.0, ALU.subtract, minus_log_dur)
 
         tanh_in = on_scalar("tanh_in", p[GATE_IN], ACT.Tanh, bias=column(half_b_sb, GATE_IN), scale=0.5)
         tanh_inbar = on_scalar(

@@ -26,17 +26,23 @@ def tile_ctlstm_kernel(tc, table, w, b, dur, offs, out):
         tc.tile_pool(name="held", bufs=1) as held,
         tc.psum_pool(name="psum", bufs=1) as psum,
     ):
-        offsets = held.tile([D, N // PER_COLUMN], U16, name="offsets")
-        nc.sync.dma_start(offsets[:], offs)
-        w_sb = held.tile([D, GATES * D], BF16, name="w_sb")
-        nc.sync.dma_start(w_sb[:], w)
         table_sb = held.tile([D, TYPES], BF16, name="table_sb")
         nc.sync.dma_start(table_sb[:], table)
-        dur_sb = held.tile([D, N], F32, name="dur_sb")
-        nc.sync.dma_start(dur_sb[:], dur.broadcast_to([D, N]))
+        offsets = held.tile([D, N // PER_COLUMN], U16, name="offsets")
+        nc.sync.dma_start(offsets[:], offs)
+        w_sb = {}
+        w_decay_sb = held.tile([D, D], BF16, name="w_decay_sb")
+        nc.sync.dma_start(w_decay_sb[:], w[:, GATE_DECAY * D : (GATE_DECAY + 1) * D])
+        w_sb[GATE_DECAY] = w_decay_sb[:]
         b_sb = held.tile([D, GATES], F32, name="b_sb")
         with nc.allow_non_contiguous_dma(reason="512 floats, one to a partition and gate"):
-            nc.scalar.dma_start(b_sb[:], b.rearrange("(g h) o -> h (g o)", g=GATES))
+            nc.sync.dma_start(b_sb[:], b.rearrange("(g h) o -> h (g o)", g=GATES))
+        w_others_sb = held.tile([D, GATE_DECAY * D], BF16, name="w_others_sb")
+        nc.sync.dma_start(w_others_sb[:], w[:, 0 : GATE_DECAY * D])
+        for g in (GATE_IN, GATE_Z, GATE_INBAR):
+            w_sb[g] = w_others_sb[:, g * D : (g + 1) * D]
+        dur_sb = held.tile([D, N], F32, name="dur_sb")
+        nc.sync.dma_start(dur_sb[:], dur.broadcast_to([D, N]))
 
         scratch = held.tile([D, 1], F32, name="scratch")
         nc.vector.memset(scratch[:], 0.0)
@@ -79,7 +85,7 @@ def tile_ctlstm_kernel(tc, table, w, b, dur, offs, out):
                 bank = psum.tile([D, PIECE], F32, name=f"p{g}_{k}")
                 columns = slice(k * PIECE // PER_COLUMN, (k + 1) * PIECE // PER_COLUMN)
                 picked = table_sb[:].indirect(offsets[:, columns])
-                nc.tensor.matmul(bank[:], w_sb[:, g * D : (g + 1) * D], picked)
+                nc.tensor.matmul(bank[:], w_sb[g], picked)
                 p[g].append(bank[:])
 
         dur_pieces = pieces_of(dur_sb)

@@ -37,12 +37,12 @@ def tile_ctlstm_kernel(tc, table, w, b, dur, offs, out):
         b_sb = held.tile([D, GATES], F32, name="b_sb")
         with nc.allow_non_contiguous_dma(reason="512 floats, one to a partition and gate"):
             nc.sync.dma_start(b_sb[:], b.rearrange("(g h) o -> h (g o)", g=GATES))
+        dur_sb = held.tile([D, N], F32, name="dur_sb")
+        nc.sync.dma_start(dur_sb[:], dur.broadcast_to([D, N]))
         w_others_sb = held.tile([D, GATE_DECAY * D], BF16, name="w_others_sb")
         nc.sync.dma_start(w_others_sb[:], w[:, 0 : GATE_DECAY * D])
         for g in (GATE_IN, GATE_Z, GATE_INBAR):
             w_sb[g] = w_others_sb[:, g * D : (g + 1) * D]
-        dur_sb = held.tile([D, N], F32, name="dur_sb")
-        nc.sync.dma_start(dur_sb[:], dur.broadcast_to([D, N]))
 
         scratch = held.tile([D, 1], F32, name="scratch")
         nc.vector.memset(scratch[:], 0.0)

@@ -9,8 +9,9 @@ GATE_IN, GATE_Z, GATE_INBAR, GATE_DECAY = 0, 1, 2, 3
 FLOPS = 2 * D * GATES * D * N
 
 PSUM_BANKS = 8
-PIECES = PSUM_BANKS // GATES
-PIECE = N // PIECES
+BOUNDS = (0, 192, 352, N)
+PIECES = len(BOUNDS) - 1
+WIDEST = max(BOUNDS[k + 1] - BOUNDS[k] for k in range(PIECES))
 
 SHIFT = 0.44068679
 Q_SCALE, Q_SHIFT, Q_REST = 0.37062380, -0.20779434, 1.18033029
@@ -24,7 +25,7 @@ def tile_ctlstm_kernel(tc, table, w, b, dur, offs, out):
     nc = tc.nc
     with (
         tc.tile_pool(name="held", bufs=1) as held,
-        tc.psum_pool(name="psum", bufs=1) as psum,
+        tc.psum_pool(name="psum", bufs=PSUM_BANKS) as psum,
     ):
         table_sb = held.tile([D, TYPES], BF16, name="table_sb")
         nc.sync.dma_start(table_sb[:], table)
@@ -55,7 +56,7 @@ def tile_ctlstm_kernel(tc, table, w, b, dur, offs, out):
             return tile[:, g : g + 1]
 
         def pieces_of(tile):
-            return [tile[:, k * PIECE : (k + 1) * PIECE] for k in range(PIECES)]
+            return [tile[:, BOUNDS[k] : BOUNDS[k + 1]] for k in range(PIECES)]
 
         def fresh(name):
             return pieces_of(held.tile([D, N], F32, name=name))
@@ -82,11 +83,12 @@ def tile_ctlstm_kernel(tc, table, w, b, dur, offs, out):
         for g in (GATE_DECAY, GATE_IN, GATE_INBAR, GATE_Z):
             p[g] = []
             for k in range(PIECES):
-                bank = psum.tile([D, PIECE], F32, name=f"p{g}_{k}")
-                columns = slice(k * PIECE // PER_COLUMN, (k + 1) * PIECE // PER_COLUMN)
+                bank = psum.tile([D, WIDEST], F32, name=f"p{g}_{k}", tag="product")
+                product = bank[:, 0 : BOUNDS[k + 1] - BOUNDS[k]]
+                columns = slice(BOUNDS[k] // PER_COLUMN, BOUNDS[k + 1] // PER_COLUMN)
                 picked = table_sb[:].indirect(offsets[:, columns])
-                nc.tensor.matmul(bank[:], w_sb[g], picked)
-                p[g].append(bank[:])
+                nc.tensor.matmul(product, w_sb[g], picked)
+                p[g].append(product)
 
         dur_pieces = pieces_of(dur_sb)
         y_abs = on_scalar("y_abs", p[GATE_DECAY], ACT.Abs, bias=column(b_sb, GATE_DECAY))
@@ -107,6 +109,11 @@ def tile_ctlstm_kernel(tc, table, w, b, dur, offs, out):
 
         faded = on_vector("faded", gap, ALU.mult, fade)
         mix = on_vector_fused("mix", tanh_inbar, ALU.add, 1.0, ALU.add, faded)
-        result = on_vector_fused("result", mix, ALU.mult, 0.5, ALU.mult, z)
+        result_sb = held.tile([D, N], F32, name="result_sb")
         for k in range(PIECES):
-            nc.sync.dma_start(out[:, k * PIECE : (k + 1) * PIECE], result[k])
+            nc.vector.scalar_tensor_tensor(
+                pieces_of(result_sb)[k], mix[k], 0.5, z[k], op0=ALU.mult, op1=ALU.mult
+            )
+        for first, behind_last in ((0, PIECES - 1), (PIECES - 1, PIECES)):
+            columns = slice(BOUNDS[first], BOUNDS[behind_last])
+            nc.sync.dma_start(out[:, columns], result_sb[:, columns])

@@ -8,10 +8,8 @@ GATES = 4
 GATE_IN, GATE_Z, GATE_INBAR, GATE_DECAY = 0, 1, 2, 3
 FLOPS = 2 * D * GATES * D * N
 
-PSUM_BANKS = 8
 BOUNDS = (0, 192, 352, N)
 PIECES = len(BOUNDS) - 1
-WIDEST = max(BOUNDS[k + 1] - BOUNDS[k] for k in range(PIECES))
 
 SHIFT = 0.44068679
 Q_SCALE, Q_SHIFT, Q_REST = 0.37062380, -0.20779434, 1.18033029
@@ -25,7 +23,7 @@ def tile_ctlstm_kernel(tc, table, w, b, dur, offs, out):
     nc = tc.nc
     with (
         tc.tile_pool(name="held", bufs=1) as held,
-        tc.psum_pool(name="psum", bufs=PSUM_BANKS) as psum,
+        tc.psum_pool(name="psum", bufs=1) as psum,
     ):
         table_sb = held.tile([D, TYPES], BF16, name="table_sb")
         nc.sync.dma_start(table_sb[:], table)
@@ -67,6 +65,11 @@ def tile_ctlstm_kernel(tc, table, w, b, dur, offs, out):
                 nc.scalar.activation(made[k], in_[k], func, bias=bias, scale=scale)
             return made
 
+        def on_scalar_whole(name, in_, func, bias=0.0, scale=1.0):
+            made = held.tile([D, N], F32, name=name)
+            nc.scalar.activation(made[:], in_, func, bias=bias, scale=scale)
+            return pieces_of(made)
+
         def on_vector(name, in0, op, in1):
             made = fresh(name)
             for k in range(PIECES):
@@ -79,16 +82,25 @@ def tile_ctlstm_kernel(tc, table, w, b, dur, offs, out):
                 nc.vector.scalar_tensor_tensor(made[k], in0[k], scalar, in1[k], op0=op0, op1=op1)
             return made
 
-        p = {}
-        for g in (GATE_DECAY, GATE_IN, GATE_INBAR, GATE_Z):
-            p[g] = []
+        def project_by_pieces(g):
+            products = []
             for k in range(PIECES):
-                bank = psum.tile([D, WIDEST], F32, name=f"p{g}_{k}", tag="product")
-                product = bank[:, 0 : BOUNDS[k + 1] - BOUNDS[k]]
+                bank = psum.tile([D, BOUNDS[k + 1] - BOUNDS[k]], F32, name=f"p{g}_{k}")
                 columns = slice(BOUNDS[k] // PER_COLUMN, BOUNDS[k + 1] // PER_COLUMN)
-                picked = table_sb[:].indirect(offsets[:, columns])
-                nc.tensor.matmul(product, w_sb[g], picked)
-                p[g].append(product)
+                nc.tensor.matmul(bank[:], w_sb[g], table_sb[:].indirect(offsets[:, columns]))
+                products.append(bank[:])
+            return products
+
+        def project_whole(g):
+            bank = psum.tile([D, N], F32, name=f"p{g}")
+            nc.tensor.matmul(bank[:], w_sb[g], table_sb[:].indirect(offsets[:]))
+            return bank[:]
+
+        p = {}
+        p[GATE_DECAY] = project_by_pieces(GATE_DECAY)
+        p[GATE_IN] = project_whole(GATE_IN)
+        p[GATE_INBAR] = project_by_pieces(GATE_INBAR)
+        p[GATE_Z] = project_whole(GATE_Z)
 
         dur_pieces = pieces_of(dur_sb)
         y_abs = on_scalar("y_abs", p[GATE_DECAY], ACT.Abs, bias=column(b_sb, GATE_DECAY))
@@ -99,13 +111,13 @@ def tile_ctlstm_kernel(tc, table, w, b, dur, offs, out):
         minus_log_dur = on_vector_fused("minus_log_dur", square, ALU.add, Q_REST, ALU.mult, minus_line_dur)
         x = on_vector_fused("x", y_dur, ALU.max, 0.0, ALU.subtract, minus_log_dur)
 
-        tanh_in = on_scalar("tanh_in", p[GATE_IN], ACT.Tanh, bias=column(half_b_sb, GATE_IN), scale=0.5)
+        tanh_in = on_scalar_whole("tanh_in", p[GATE_IN], ACT.Tanh, bias=column(half_b_sb, GATE_IN), scale=0.5)
         tanh_inbar = on_scalar(
             "tanh_inbar", p[GATE_INBAR], ACT.Tanh, bias=column(half_b_sb, GATE_INBAR), scale=0.5
         )
         gap = on_vector("gap", tanh_in, ALU.subtract, tanh_inbar)
         fade = on_scalar("fade", x, ACT.Exp, scale=-1.0)
-        z = on_scalar("z", p[GATE_Z], ACT.Tanh, bias=column(b_sb, GATE_Z))
+        z = on_scalar_whole("z", p[GATE_Z], ACT.Tanh, bias=column(b_sb, GATE_Z))
 
         faded = on_vector("faded", gap, ALU.mult, fade)
         mix = on_vector_fused("mix", tanh_inbar, ALU.add, 1.0, ALU.add, faded)

import concourse.mybir as mybir

D = 128
TYPES = 1024
N = 512
PER_COLUMN = 16
GATES = 4
GATE_IN, GATE_Z, GATE_INBAR, GATE_DECAY = 0, 1, 2, 3
FLOPS = 2 * D * GATES * D * N

BOUNDS = (0, 192, 352, N)
PIECES = len(BOUNDS) - 1

SHIFT = 0.44068679
Q_SCALE, Q_SHIFT, Q_REST = 0.37062380, -0.20779434, 1.18033029

BF16, F32, U16 = mybir.dt.bfloat16, mybir.dt.float32, mybir.dt.uint16
ACT = mybir.ActivationFunctionType
ALU = mybir.AluOpType


def tile_ctlstm_kernel(tc, table, w, b, dur, offs, out):
    nc = tc.nc
    with (
        tc.tile_pool(name="held", bufs=1) as held,
        tc.psum_pool(name="psum", bufs=1) as psum,
    ):
        table_sb = held.tile([D, TYPES], BF16, name="table_sb")
        nc.sync.dma_start(table_sb[:], table)
        offsets = held.tile([D, N // PER_COLUMN], U16, name="offsets")
        nc.sync.dma_start(offsets[:], offs)
        w_sb = {}
        w_decay_sb = held.tile([D, D], BF16, name="w_decay_sb")
        nc.sync.dma_start(w_decay_sb[:], w[:, GATE_DECAY * D : (GATE_DECAY + 1) * D])
        w_sb[GATE_DECAY] = w_decay_sb[:]
        b_sb = held.tile([D, GATES], F32, name="b_sb")
        with nc.allow_non_contiguous_dma(reason="512 floats, one to a partition and gate"):
            nc.sync.dma_start(b_sb[:], b.rearrange("(g h) o -> h (g o)", g=GATES))
        dur_sb = held.tile([D, N], F32, name="dur_sb")
        nc.sync.dma_start(dur_sb[:], dur.broadcast_to([D, N]))
        w_others_sb = held.tile([D, GATE_DECAY * D], BF16, name="w_others_sb")
        nc.sync.dma_start(w_others_sb[:], w[:, 0 : GATE_DECAY * D])
        for g in (GATE_IN, GATE_Z, GATE_INBAR):
            w_sb[g] = w_others_sb[:, g * D : (g + 1) * D]

        scratch = held.tile([D, 1], F32, name="scratch")
        nc.vector.memset(scratch[:], 0.0)
        nc.scalar.activation(scratch[:], scratch[:], ACT.Exp)

        half_b_sb = held.tile([D, GATES], F32, name="half_b_sb")
        nc.vector.tensor_scalar_mul(half_b_sb[:], b_sb[:], 0.5)

        def column(tile, g):
            return tile[:, g : g + 1]

        def pieces_of(tile):
            return [tile[:, BOUNDS[k] : BOUNDS[k + 1]] for k in range(PIECES)]

        def fresh(name):
            return pieces_of(held.tile([D, N], F32, name=name))

        def on_scalar(name, in_, func, bias=0.0, scale=1.0):
            made = fresh(name)
            for k in range(PIECES):
                nc.scalar.activation(made[k], in_[k], func, bias=bias, scale=scale)
            return made

        def on_scalar_whole(name, in_, func, bias=0.0, scale=1.0):
            made = held.tile([D, N], F32, name=name)
            nc.scalar.activation(made[:], in_, func, bias=bias, scale=scale)
            return pieces_of(made)

        def on_vector(name, in0, op, in1):
            made = fresh(name)
            for k in range(PIECES):
                nc.vector.tensor_tensor(made[k], in0[k], in1[k], op)
            return made

        def on_vector_fused(name, in0, op0, scalar, op1, in1):
            made = fresh(name)
            for k in range(PIECES):
                nc.vector.scalar_tensor_tensor(made[k], in0[k], scalar, in1[k], op0=op0, op1=op1)
            return made

        def project_by_pieces(g):
            products = []
            for k in range(PIECES):
                bank = psum.tile([D, BOUNDS[k + 1] - BOUNDS[k]], F32, name=f"p{g}_{k}")
                columns = slice(BOUNDS[k] // PER_COLUMN, BOUNDS[k + 1] // PER_COLUMN)
                nc.tensor.matmul(bank[:], w_sb[g], table_sb[:].indirect(offsets[:, columns]))
                products.append(bank[:])
            return products

        def project_whole(g):
            bank = psum.tile([D, N], F32, name=f"p{g}")
            nc.tensor.matmul(bank[:], w_sb[g], table_sb[:].indirect(offsets[:]))
            return bank[:]

        p = {}
        p[GATE_DECAY] = project_by_pieces(GATE_DECAY)
        p[GATE_IN] = project_whole(GATE_IN)
        p[GATE_INBAR] = project_by_pieces(GATE_INBAR)
        p[GATE_Z] = project_whole(GATE_Z)

        dur_pieces = pieces_of(dur_sb)
        y_abs = on_scalar("y_abs", p[GATE_DECAY], ACT.Abs, bias=column(b_sb, GATE_DECAY))
        y_dur = on_vector_fused("y_dur", p[GATE_DECAY], ALU.add, column(b_sb, GATE_DECAY), ALU.mult, dur_pieces)
        tau = on_scalar("tau", y_abs, ACT.Tanh, bias=SHIFT, scale=0.5)
        square = on_scalar("square", tau, ACT.Square, bias=Q_SHIFT, scale=Q_SCALE)
        minus_line_dur = on_vector_fused("minus_line_dur", tau, ALU.add, -1.0, ALU.mult, dur_pieces)
        minus_log_dur = on_vector_fused("minus_log_dur", square, ALU.add, Q_REST, ALU.mult, minus_line_dur)
        x = on_vector_fused("x", y_dur, ALU.max, 0.0, ALU.subtract, minus_log_dur)

        tanh_in = on_scalar_whole("tanh_in", p[GATE_IN], ACT.Tanh, bias=column(half_b_sb, GATE_IN), scale=0.5)
        tanh_inbar = on_scalar(
            "tanh_inbar", p[GATE_INBAR], ACT.Tanh, bias=column(half_b_sb, GATE_INBAR), scale=0.5
        )
        gap = on_vector("gap", tanh_in, ALU.subtract, tanh_inbar)
        fade = on_scalar("fade", x, ACT.Exp, scale=-1.0)
        z = on_scalar_whole("z", p[GATE_Z], ACT.Tanh, bias=column(b_sb, GATE_Z))

        faded = on_vector("faded", gap, ALU.mult, fade)
        mix = on_vector_fused("mix", tanh_inbar, ALU.add, 1.0, ALU.add, faded)
        result_sb = held.tile([D, N], F32, name="result_sb")
        for k in range(PIECES):
            nc.vector.scalar_tensor_tensor(
                pieces_of(result_sb)[k], mix[k], 0.5, z[k], op0=ALU.mult, op1=ALU.mult
            )
        for first, behind_last in ((0, PIECES - 1), (PIECES - 1, PIECES)):
            columns = slice(BOUNDS[first], BOUNDS[behind_last])
            nc.sync.dma_start(out[:, columns], result_sb[:, columns])
